import numpy as np
import ml_dtypes


def mxq(x, axis, fmt="e4m3"):
    dtype, down = {"e4m3": (ml_dtypes.float8_e4m3fn, 7), "e5m2": (ml_dtypes.float8_e5m2, 14)}[fmt]
    v = np.moveaxis(np.asarray(x, np.float32).astype(ml_dtypes.bfloat16).astype(np.float64), axis, -1)
    blocks = v.reshape(v.shape[:-1] + (-1, 32))
    amax = np.abs(blocks).max(-1, keepdims=True)
    byte = np.maximum(np.where(amax > 0, np.frexp(amax)[1] - 1 + 127, 0) - down, 1)
    scale = np.exp2(byte - 127.0)
    codes = (blocks / scale).astype(np.float32).astype(dtype).astype(np.float64)
    return np.moveaxis((codes * scale).reshape(v.shape), -1, axis)


WIDE = False


def mx_kscale(k):
    if not WIDE:
        return np.ones(k)
    levels = np.array([30, -30])
    if k % 512:
        return np.exp2(np.random.permutation(np.resize(levels, k // 32))).repeat(32)
    a = np.empty((k // 512, 16))
    for p in range(k // 512):
        a[p, :8] = np.random.permutation(np.resize(levels, 8))
        for g in range(8):
            far = levels[np.abs(levels - a[p, g]) >= 10]
            a[p, g + 8] = far[np.random.randint(len(far))]
    return np.exp2(a.ravel()).repeat(32)


BF16 = ml_dtypes.bfloat16


def bf(x):
    return np.asarray(x, np.float32).astype(BF16)


def f64(x):
    return np.asarray(x).astype(np.float64)


B, S, DIM, H, NKV, HD, GS = 1, 512, 2048, 16, 4, 128, 128
QS = H * HD
KVS = NKV * HD
HALF = HD // 2
ROPE_BASE = 10000.0
RMS_EPS = 1.1920929e-07


def rms_norm(v):
    return v / np.sqrt(np.mean(v * v, axis=-1, keepdims=True) + RMS_EPS)


def rope_cos_sin():
    inv_freq = 1.0 / ROPE_BASE ** (np.arange(0, HD, 2) / HD)
    freqs = np.outer(np.arange(S), inv_freq)
    return np.cos(freqs)[None, :, None, :], np.sin(freqs)[None, :, None, :]


def apply_rotary_emb(u, cos, sin):
    u1, u2 = u[..., :HALF], u[..., HALF:]
    return np.concatenate((u1 * cos + u2 * sin, u1 * -sin + u2 * cos), axis=-1)


def setup_inputs():
    s = mx_kscale(DIM)
    return {"x": bf(np.random.standard_normal((B, S, DIM)) * s),
            "w_qkv_tern": bf(np.random.standard_normal((QS + 2 * KVS, DIM)) * 0.66 / np.sqrt(DIM) / s[None, :]),
            "q_gain": bf(1.0 + 0.1 * np.random.standard_normal(H))}


def reference(x, w_qkv_tern, q_gain):
    qkv = mxq(f64(x), 2, "e5m2") @ mxq(f64(w_qkv_tern), 1, "e4m3").T
    q = qkv[..., :QS].reshape(B, S, H, HD)
    k = qkv[..., QS:QS + KVS].reshape(B, S, NKV, HD)
    v = qkv[..., QS + KVS:].reshape(B, S, NKV, HD)
    q, k = rms_norm(q), rms_norm(k)
    cos, sin = rope_cos_sin()
    q = apply_rotary_emb(q, cos, sin)
    k = apply_rotary_emb(k, cos, sin)
    q = q * f64(q_gain)[None, None, :, None]
    return q, k, v

@@ -1,0 +1,287 @@
+import math
+from contextlib import ExitStack
+
+import concourse.mybir as mybir
+from concourse.masks import make_identity
+
+S, DIM, HD = 512, 2048, 128
+Q_COLS, K_COLS, V_COLS = 2048, 512, 512
+ROPE_BASE = 10000.0
+RMS_EPS = 1.1920929e-07
+FLOPS = 2 * S * DIM * (Q_COLS + K_COLS + V_COLS)
+
+F32 = mybir.dt.float32
+BF16 = mybir.dt.bfloat16
+I32 = mybir.dt.int32
+U32 = mybir.dt.uint32
+U8 = mybir.dt.uint8
+E5M2 = mybir.dt.float8_e5m2_x4
+E4M3 = mybir.dt.float8_e4m3fn_x4
+ALU = mybir.AluOpType
+ACT = mybir.ActivationFunctionType
+
+P = 128
+HALF = HD // 2
+K_PASS = 512
+PASSES = DIM // K_PASS
+PANEL = 256
+X_PANELS = S // PANEL
+Q_PANELS = Q_COLS // PANEL
+QK_PANELS = (Q_COLS + K_COLS) // PANEL
+W_PANELS = (Q_COLS + K_COLS + V_COLS) // PANEL
+TOKEN_TILES = S // P
+SPLIT_LOADS = 4
+
+
+def tile_causalselfattention_pa_kernel(tc, x, w_qkv_tern, q_gain, out_0, out_1, out_2):
+    nc = tc.nc
+    x_rows = x.rearrange("b s k -> (b s) k")
+    q_out = out_0.rearrange("b s h d -> (b s) (h d)")
+    k_out = out_1.rearrange("b s h d -> (b s) (h d)")
+    v_out = out_2.rearrange("b s h d -> (b s) (h d)")
+
+    with ExitStack() as ctx:
+        keep = ctx.enter_context(tc.tile_pool(name="keep", bufs=1))
+        work = ctx.enter_context(tc.tile_pool(name="work", bufs=3))
+        psum = ctx.enter_context(tc.psum_pool(name="psum", bufs=1))
+        ctx.enter_context(tc.manual_schedule())
+
+        def load_panel(name, rows, pieces):
+            width = DIM // pieces
+            tiles = []
+            for c in range(pieces):
+                piece = keep.tile([P, 2, width], BF16, name="%s_%d" % (name, c))
+                nc.sync.dma_start(
+                    out=piece[:],
+                    in_=rows[:, c * width : (c + 1) * width].rearrange("(t p) k -> p t k", p=P),
+                )
+                tiles.append(piece)
+            return tiles
+
+        sources = [("x%d" % a, x_rows[a * PANEL : (a + 1) * PANEL, :]) for a in range(X_PANELS)]
+        sources += [("w%d" % s, w_qkv_tern[s * PANEL : (s + 1) * PANEL, :]) for s in range(W_PANELS)]
+        raw = []
+        gain = keep.tile([P, Q_COLS // HD], BF16)
+        for i, (name, rows) in enumerate(sources):
+            if i == SPLIT_LOADS:
+                nc.sync.dma_start(out=gain[:], in_=q_gain.partition_broadcast(P))
+            raw.append(load_panel(name, rows, 2 if i < SPLIT_LOADS else 1))
+
+        position = keep.tile([P, TOKEN_TILES], I32)
+        nc.gpsimd.iota(position[:], pattern=[[P, TOKEN_TILES]], base=0, channel_multiplier=1)
+        identity = keep.tile([P, P], F32)
+        make_identity(nc, identity[:])
+
+        ratio = ROPE_BASE ** (-2.0 / HD)
+        fine = keep.tile([P, TOKEN_TILES, 8], F32)
+        for lo in range(8):
+            nc.vector.tensor_scalar(
+                out=fine[:, :, lo], in0=position[:], scalar1=ratio**lo / (2 * math.pi), scalar2=None, op0=ALU.mult
+            )
+        turns = keep.tile([P, TOKEN_TILES, 2, HALF], F32)
+        for hi in range(8):
+            nc.vector.tensor_scalar(
+                out=turns[:, :, 0, 8 * hi : 8 * hi + 8], in0=fine[:], scalar1=ratio ** (8 * hi), scalar2=None, op0=ALU.mult
+            )
+        nc.vector.tensor_scalar(out=turns[:, :, 1, :], in0=turns[:, :, 0, :], scalar1=-0.25, scalar2=None, op0=ALU.add)
+        whole = keep.tile([P, TOKEN_TILES, 2, HALF], I32)
+        nc.vector.tensor_copy(out=whole[:], in_=turns[:])
+        fraction = keep.tile([P, TOKEN_TILES, 2, HALF], F32)
+        nc.vector.tensor_tensor(out=fraction[:], in0=turns[:], in1=whole[:], op=ALU.subtract)
+        half_sine = keep.tile([P, TOKEN_TILES * 2, HALF], F32)
+        nc.scalar.activation(
+            out=half_sine[:], in_=fraction[:].rearrange("p t c j -> p (t c) j"), func=ACT.Sin, scale=math.pi
+        )
+        doubled = keep.tile([P, TOKEN_TILES * 2, HALF], F32)
+        table = keep.tile([P, TOKEN_TILES, 2, HD], F32)
+
+        def finish_table():
+            nc.vector.scalar_tensor_tensor(
+                out=doubled[:], in0=half_sine[:], scalar=-2.0, in1=half_sine[:], op0=ALU.mult, op1=ALU.mult
+            )
+            nc.vector.tensor_scalar(
+                out=table[:].rearrange("p t c (d j) -> p (t c) d j", d=2),
+                in0=doubled[:].unsqueeze(2).to_broadcast([P, TOKEN_TILES * 2, 2, HALF]),
+                scalar1=1.0,
+                scalar2=None,
+                op0=ALU.add,
+            )
+
+        def transpose_panel(i):
+            banks = []
+            for g in range(PASSES):
+                bank = psum.tile([P, 2, 2, P], F32, name="turned%d" % g)
+                per_piece = PASSES // len(raw[i])
+                piece = raw[i][g // per_piece]
+                first = 256 * (g % per_piece)
+                for t in range(2):
+                    words = piece[:, t, :].bitcast(F32)
+                    for u in range(2):
+                        nc.tensor.transpose(bank[:, t, u, :], words[:, first + u : first + 256 : 2], identity[:])
+                banks.append(bank)
+            return banks
+
+        def copy_out(bank, on_vector):
+            staged = work.tile([P, 4 * PANEL], BF16, name="staged", bufs=6, align_bytes=64)
+            dst = staged[:].bitcast(F32).rearrange("p (t r u) -> p t r u", t=2, u=2)
+            src = bank[:].rearrange("p t u r -> p t r u")
+            if on_vector:
+                nc.vector.tensor_copy(out=dst, in_=src)
+            else:
+                nc.scalar.copy(out=dst, in_=src)
+            return staged
+
+        def new_operand(pool, name):
+            codes = pool.tile([P, PASSES, PANEL], U32, name=name + "_codes", align_bytes=64)
+            scales = pool.tile([P, PASSES, PANEL], U8, name=name + "_scales", align_bytes=64)
+            return codes, scales
+
+        def quantize(operand, g, staged, fmt):
+            codes, scales = operand
+            nc.vector.quantize_mx(out=codes[:, g, :].bitcast(fmt), scales=scales[:, g, :], in_=staged[:])
+
+        def prepare_panel(i, operand, fmt):
+            banks = transpose_panel(i)
+            for g in range(PASSES):
+                quantize(operand, g, copy_out(banks[g], False), fmt)
+
+        x_ops = [new_operand(keep, "x%d" % a) for a in range(X_PANELS)]
+        w_ops = {}
+        for a in range(X_PANELS):
+            prepare_panel(a, x_ops[a], E5M2)
+        finish_table()
+        w_ops[0] = new_operand(work, "w")
+        prepare_panel(X_PANELS, w_ops[0], E4M3)
+
+        def multiply(s, a):
+            acc = psum.tile([P, 2, PANEL], F32, name="acc%d" % (2 * (s % 2) + a))
+            x_codes, x_scales = x_ops[a]
+            w_codes, w_scales = w_ops[s]
+            for t in range(2):
+                tokens = slice(t * P, (t + 1) * P)
+                for g in range(PASSES):
+                    nc.tensor.matmul_mx(
+                        out=acc[:, t, :],
+                        lhsT=x_codes[:, g, tokens].bitcast(E5M2),
+                        lhsT_scale=x_scales[:, g, tokens],
+                        rhs=w_codes[:, g, :].bitcast(E4M3),
+                        rhs_scale=w_scales[:, g, :],
+                        start=(g == 0),
+                        stop=(g == PASSES - 1),
+                    )
+            return {"s": s, "a": a, "acc": acc, "normed": s < QK_PANELS}
+
+        def sum_squares(job):
+            if not job["normed"]:
+                return
+            squares = work.tile([P, 4, HD], BF16, name="squares")
+            job["sums"] = work.tile([P, 4], F32, name="sums")
+            heads = job["acc"][:].rearrange("p t (h d) -> p (t h) d", d=HD)
+            for c in range(4):
+                nc.scalar.activation(
+                    out=squares[:, c, :], in_=heads[:, c, :], func=ACT.Square, accum_out=job["sums"][:, c : c + 1]
+                )
+
+        def inverse_rms(job):
+            if not job["normed"]:
+                return
+            job["factor"] = work.tile([P, 4], F32, name="inv_rms")
+            nc.scalar.activation(
+                out=job["factor"][:], in_=job["sums"][:], func=ACT.Abs_reciprocal_sqrt, scale=1.0 / HD, bias=RMS_EPS
+            )
+
+        def apply_gain(job):
+            if job["s"] >= Q_PANELS:
+                return
+            gained = work.tile([P, 2, 2], F32, name="gained")
+            s = job["s"]
+            nc.vector.tensor_tensor(
+                out=gained[:],
+                in0=job["factor"][:].rearrange("p (t h) -> p t h", t=2),
+                in1=gain[:, 2 * s : 2 * s + 2].unsqueeze(1).to_broadcast([P, 2, 2]),
+                op=ALU.mult,
+            )
+            job["factor"] = gained[:].rearrange("p t h -> p (t h)")
+
+        def rotate_products(job):
+            job["result"] = keep.tile([P, 2, PANEL], F32, name="result%d_%d" % (job["s"], job["a"]))
+            if not job["normed"]:
+                if job["a"] == 0:
+                    nc.scalar.copy(out=job["result"][:], in_=job["acc"][:])
+                else:
+                    nc.vector.tensor_copy(out=job["result"][:], in_=job["acc"][:])
+                return
+            job["terms"] = work.tile([P, 4, 2, HD], F32, name="terms")
+            heads = job["acc"][:].rearrange("p t (h d) -> p (t h) d", d=HD)
+            for c in range(4):
+                nc.vector.scalar_tensor_tensor(
+                    out=job["terms"][:, c, :, :],
+                    in0=heads[:, c, :].unsqueeze(1).to_broadcast([P, 2, HD]),
+                    scalar=job["factor"][:, c : c + 1],
+                    in1=table[:, 2 * job["a"] + c // 2, :, :],
+                    op0=ALU.mult,
+                    op1=ALU.mult,
+                )
+
+        def add_and_store(job):
+            s, a = job["s"], job["a"]
+            if job["normed"]:
+                terms = job["terms"][:].rearrange("p c f (e j) -> p c (f e) j", e=2)
+                halves = job["result"][:].rearrange("p t (h e j) -> p (t h) e j", h=2, e=2)
+                nc.vector.tensor_tensor(out=halves[:, :, 0, :], in0=terms[:, :, 0, :], in1=terms[:, :, 3, :], op=ALU.add)
+                nc.vector.tensor_tensor(
+                    out=halves[:, :, 1, :], in0=terms[:, :, 1, :], in1=terms[:, :, 2, :], op=ALU.subtract
+                )
+            if s < Q_PANELS:
+                target, column = q_out, s * PANEL
+            elif s < QK_PANELS:
+                target, column = k_out, (s - Q_PANELS) * PANEL
+            else:
+                target, column = v_out, (s - QK_PANELS) * PANEL
+            nc.sync.dma_start(
+                out=target[a * PANEL : (a + 1) * PANEL, column : column + PANEL].rearrange("(t p) c -> p t c", p=P),
+                in_=job["result"][:],
+            )
+
+        early = late = None
+        for s in range(W_PANELS + 1):
+            ahead = s + 1 < W_PANELS
+            on_vector = False
+            staged = []
+            if ahead:
+                banks = transpose_panel(X_PANELS + s + 1)
+                w_ops[s + 1] = new_operand(work, "w")
+
+            def stage(g):
+                if ahead:
+                    staged.append(copy_out(banks[g], on_vector))
+
+            def quantize_ahead(g):
+                if ahead:
+                    quantize(w_ops[s + 1], g, staged[g], E4M3)
+
+            if late:
+                sum_squares(late)
+            stage(0)
+            if late:
+                inverse_rms(late)
+            stage(1)
+            if late:
+                apply_gain(late)
+                add_and_store(early)
+                rotate_products(late)
+            quantize_ahead(0)
+            quantize_ahead(1)
+            stage(2)
+            stage(3)
+            if late:
+                add_and_store(late)
+            quantize_ahead(2)
+            if s < W_PANELS:
+                early = multiply(s, 0)
+                late = multiply(s, 1)
+                sum_squares(early)
+                inverse_rms(early)
+                apply_gain(early)
+                quantize_ahead(3)
+                rotate_products(early)

@@ -58,19 +58,22 @@ def tile_causalselfattention_pa_kernel(tc, x, w_qkv_tern, q_gain, out_0, out_1, 
                 tiles.append(piece)
             return tiles
 
-        sources = [("x%d" % a, x_rows[a * PANEL : (a + 1) * PANEL, :]) for a in range(X_PANELS)]
-        sources += [("w%d" % s, w_qkv_tern[s * PANEL : (s + 1) * PANEL, :]) for s in range(W_PANELS)]
-        raw = []
-        gain = keep.tile([P, Q_COLS // HD], BF16)
-        for i, (name, rows) in enumerate(sources):
-            if i == SPLIT_LOADS:
-                nc.sync.dma_start(out=gain[:], in_=q_gain.partition_broadcast(P))
-            raw.append(load_panel(name, rows, 2 if i < SPLIT_LOADS else 1))
+        sources = {"x%d" % a: x_rows[a * PANEL : (a + 1) * PANEL, :] for a in range(X_PANELS)}
+        for s in range(W_PANELS):
+            sources["w%d" % s] = w_qkv_tern[s * PANEL : (s + 1) * PANEL, :]
+        raw = {}
+        gain_raw = keep.tile([P, Q_COLS // HD], BF16)
+        for i, name in enumerate(["x0", "w0", "x1"] + ["w%d" % s for s in range(1, W_PANELS)]):
+            if i == SPLIT_LOADS - 1:
+                nc.sync.dma_start(out=gain_raw[:], in_=q_gain.partition_broadcast(P))
+            raw[name] = load_panel(name, sources[name], 2 if i < SPLIT_LOADS else 1)
 
         position = keep.tile([P, TOKEN_TILES], I32)
         nc.gpsimd.iota(position[:], pattern=[[P, TOKEN_TILES]], base=0, channel_multiplier=1)
         identity = keep.tile([P, P], F32)
         make_identity(nc, identity[:])
+        gain = keep.tile([P, Q_COLS // HD], F32)
+        nc.gpsimd.tensor_copy(out=gain[:], in_=gain_raw[:])
 
         ratio = ROPE_BASE ** (-2.0 / HD)
         fine = keep.tile([P, TOKEN_TILES, 8], F32)
@@ -121,54 +124,66 @@ def tile_causalselfattention_pa_kernel(tc, x, w_qkv_tern, q_gain, out_0, out_1, 
                 banks.append(bank)
             return banks
 
-        def copy_out(bank, on_vector):
-            staged = work.tile([P, 4 * PANEL], BF16, name="staged", bufs=6, align_bytes=64)
-            dst = staged[:].bitcast(F32).rearrange("p (t r u) -> p t r u", t=2, u=2)
+        def new_staged():
+            return work.tile([P, 2, 4 * PANEL], BF16, name="staged", bufs=4, align_bytes=64)
+
+        def copy_out(bank, staged, g, on_vector):
+            dst = staged[:, g % 2, :].bitcast(F32).rearrange("p (t r u) -> p t r u", t=2, u=2)
             src = bank[:].rearrange("p t u r -> p t r u")
             if on_vector:
                 nc.vector.tensor_copy(out=dst, in_=src)
             else:
                 nc.scalar.copy(out=dst, in_=src)
-            return staged
 
         def new_operand(pool, name):
             codes = pool.tile([P, PASSES, PANEL], U32, name=name + "_codes", align_bytes=64)
             scales = pool.tile([P, PASSES, PANEL], U8, name=name + "_scales", align_bytes=64)
             return codes, scales
 
-        def quantize(operand, g, staged, fmt):
+        def quantize(operand, pair, staged, fmt):
             codes, scales = operand
-            nc.vector.quantize_mx(out=codes[:, g, :].bitcast(fmt), scales=scales[:, g, :], in_=staged[:])
+            both = slice(2 * pair, 2 * pair + 2)
+            nc.vector.quantize_mx(
+                out=codes[:, both, :].rearrange("p g n -> p (g n)").bitcast(fmt),
+                scales=scales[:, both, :].rearrange("p g n -> p (g n)"),
+                in_=staged[:].rearrange("p g n -> p (g n)"),
+            )
 
-        def prepare_panel(i, operand, fmt):
-            banks = transpose_panel(i)
-            for g in range(PASSES):
-                quantize(operand, g, copy_out(banks[g], False), fmt)
+        def prepare_panel(name, operand, fmt, on_vector):
+            banks = transpose_panel(name)
+            for pair in range(2):
+                staged = new_staged()
+                for g in (2 * pair, 2 * pair + 1):
+                    copy_out(banks[g], staged, g, on_vector)
+                quantize(operand, pair, staged, fmt)
 
         x_ops = [new_operand(keep, "x%d" % a) for a in range(X_PANELS)]
         w_ops = {}
-        for a in range(X_PANELS):
-            prepare_panel(a, x_ops[a], E5M2)
-        finish_table()
+        prepare_panel("x0", x_ops[0], E5M2, False)
         w_ops[0] = new_operand(work, "w")
-        prepare_panel(X_PANELS, w_ops[0], E4M3)
+        prepare_panel("w0", w_ops[0], E4M3, False)
+        finish_table()
+        prepare_panel("x1", x_ops[1], E5M2, False)
+
+        def multiply_tile(acc, s, tile):
+            x_codes, x_scales = x_ops[tile // 2]
+            w_codes, w_scales = w_ops[s]
+            tokens = slice(tile % 2 * P, (tile % 2 + 1) * P)
+            for g in range(PASSES):
+                nc.tensor.matmul_mx(
+                    out=acc,
+                    lhsT=x_codes[:, g, tokens].bitcast(E5M2),
+                    lhsT_scale=x_scales[:, g, tokens],
+                    rhs=w_codes[:, g, :].bitcast(E4M3),
+                    rhs_scale=w_scales[:, g, :],
+                    start=(g == 0),
+                    stop=(g == PASSES - 1),
+                )
 
         def multiply(s, a):
             acc = psum.tile([P, 2, PANEL], F32, name="acc%d" % (2 * (s % 2) + a))
-            x_codes, x_scales = x_ops[a]
-            w_codes, w_scales = w_ops[s]
             for t in range(2):
-                tokens = slice(t * P, (t + 1) * P)
-                for g in range(PASSES):
-                    nc.tensor.matmul_mx(
-                        out=acc[:, t, :],
-                        lhsT=x_codes[:, g, tokens].bitcast(E5M2),
-                        lhsT_scale=x_scales[:, g, tokens],
-                        rhs=w_codes[:, g, :].bitcast(E4M3),
-                        rhs_scale=w_scales[:, g, :],
-                        start=(g == 0),
-                        stop=(g == PASSES - 1),
-                    )
+                multiply_tile(acc[:, t, :], s, 2 * a + t)
             return {"s": s, "a": a, "acc": acc, "normed": s < QK_PANELS}
 
         def sum_squares(job):
@@ -194,13 +209,12 @@ def tile_causalselfattention_pa_kernel(tc, x, w_qkv_tern, q_gain, out_0, out_1, 
             if job["s"] >= Q_PANELS:
                 return
             gained = work.tile([P, 2, 2], F32, name="gained")
-            s = job["s"]
-            nc.vector.tensor_tensor(
-                out=gained[:],
-                in0=job["factor"][:].rearrange("p (t h) -> p t h", t=2),
-                in1=gain[:, 2 * s : 2 * s + 2].unsqueeze(1).to_broadcast([P, 2, 2]),
-                op=ALU.mult,
-            )
+            factor = job["factor"][:].rearrange("p (t h) -> p t h", t=2)
+            for h in range(2):
+                head = 2 * job["s"] + h
+                nc.scalar.activation(
+                    out=gained[:, :, h], in_=factor[:, :, h], func=ACT.Copy, scale=gain[:, head : head + 1]
+                )
             job["factor"] = gained[:].rearrange("p t h -> p (t h)")
 
         def rotate_products(job):
@@ -228,8 +242,8 @@ def tile_causalselfattention_pa_kernel(tc, x, w_qkv_tern, q_gain, out_0, out_1, 
             if job["normed"]:
                 terms = job["terms"][:].rearrange("p c f (e j) -> p c (f e) j", e=2)
                 halves = job["result"][:].rearrange("p t (h e j) -> p (t h) e j", h=2, e=2)
-                nc.vector.tensor_tensor(out=halves[:, :, 0, :], in0=terms[:, :, 0, :], in1=terms[:, :, 3, :], op=ALU.add)
-                nc.vector.tensor_tensor(
+                nc.gpsimd.tensor_tensor(out=halves[:, :, 0, :], in0=terms[:, :, 0, :], in1=terms[:, :, 3, :], op=ALU.add)
+                nc.gpsimd.tensor_tensor(
                     out=halves[:, :, 1, :], in0=terms[:, :, 1, :], in1=terms[:, :, 2, :], op=ALU.subtract
                 )
             if s < Q_PANELS:
@@ -243,45 +257,54 @@ def tile_causalselfattention_pa_kernel(tc, x, w_qkv_tern, q_gain, out_0, out_1, 
                 in_=job["result"][:],
             )
 
-        early = late = None
-        for s in range(W_PANELS + 1):
+        def statistics(job):
+            sum_squares(job)
+            inverse_rms(job)
+            apply_gain(job)
+
+        early = multiply(0, 0)
+        statistics(early)
+        w_ops[1] = new_operand(work, "w")
+        prepare_panel("w1", w_ops[1], E4M3, True)
+        late = multiply(0, 1)
+        for s in range(1, W_PANELS):
             ahead = s + 1 < W_PANELS
-            on_vector = False
-            staged = []
             if ahead:
-                banks = transpose_panel(X_PANELS + s + 1)
+                banks = transpose_panel("w%d" % (s + 1))
                 w_ops[s + 1] = new_operand(work, "w")
+                staged = [new_staged(), new_staged()]
 
             def stage(g):
                 if ahead:
-                    staged.append(copy_out(banks[g], on_vector))
+                    copy_out(banks[g], staged[g // 2], g, False)
 
-            def quantize_ahead(g):
+            def quantize_ahead(pair):
                 if ahead:
-                    quantize(w_ops[s + 1], g, staged[g], E4M3)
+                    quantize(w_ops[s + 1], pair, staged[pair], E4M3)
 
-            if late:
-                sum_squares(late)
+            rotate_products(early)
+            add_and_store(early)
+            sum_squares(late)
             stage(0)
-            if late:
-                inverse_rms(late)
+            inverse_rms(late)
             stage(1)
-            if late:
-                apply_gain(late)
-                add_and_store(early)
-                rotate_products(late)
-            quantize_ahead(0)
-            quantize_ahead(1)
+            apply_gain(late)
             stage(2)
             stage(3)
-            if late:
-                add_and_store(late)
-            quantize_ahead(2)
-            if s < W_PANELS:
-                early = multiply(s, 0)
+            quantize_ahead(0)
+            rotate_products(late)
+            add_and_store(late)
+            quantize_ahead(1)
+            early = multiply(s, 0)
+            if ahead:
                 late = multiply(s, 1)
-                sum_squares(early)
-                inverse_rms(early)
-                apply_gain(early)
-                quantize_ahead(3)
-                rotate_products(early)
+                statistics(early)
+
+        rotate_products(early)
+        add_and_store(early)
+        for tile in (2, 3):
+            acc = psum.tile([P, PANEL], F32, name="turned%d" % tile)
+            multiply_tile(acc[:], W_PANELS - 1, tile)
+            result = keep.tile([P, PANEL], F32, name="last%d" % tile)
+            nc.vector.tensor_copy(out=result[:], in_=acc[:])
+            nc.sync.dma_start(out=v_out[tile * P : (tile + 1) * P, V_COLS - PANEL :], in_=result[:])

@@ -21,16 +21,22 @@ ALU = mybir.AluOpType
 ACT = mybir.ActivationFunctionType
 
 P = 128
-HALF = HD // 2
-K_PASS = 512
-PASSES = DIM // K_PASS
-PANEL = 256
-X_PANELS = S // PANEL
-Q_PANELS = Q_COLS // PANEL
-QK_PANELS = (Q_COLS + K_COLS) // PANEL
-W_PANELS = (Q_COLS + K_COLS + V_COLS) // PANEL
+FREQS = HD // 2
+PASSES = DIM // 512
+PASS_WORDS = 256
+K_HALF = DIM // 2
+PANEL = 2 * P
 TOKEN_TILES = S // P
-SPLIT_LOADS = 4
+Q_PANELS = Q_COLS // PANEL
+NORMED_PANELS = (Q_COLS + K_COLS) // PANEL
+W_PANELS = (Q_COLS + K_COLS + V_COLS) // PANEL
+VECTORS = 4
+
+BY_ROWS = [(0, 0), (0, 1), (1, 0), (1, 1)]
+BY_HALVES = [(0, 0), (1, 0), (0, 1), (1, 1)]
+
+STAGED_BUFS = 4
+RESULT_BUFS = 12
 
 
 def tile_causalselfattention_pa_kernel(tc, x, w_qkv_tern, q_gain, out_0, out_1, out_2):
@@ -46,34 +52,34 @@ def tile_causalselfattention_pa_kernel(tc, x, w_qkv_tern, q_gain, out_0, out_1, 
         psum = ctx.enter_context(tc.psum_pool(name="psum", bufs=1))
         ctx.enter_context(tc.manual_schedule())
 
-        def load_panel(name, rows, pieces):
-            width = DIM // pieces
-            tiles = []
-            for c in range(pieces):
-                piece = keep.tile([P, 2, width], BF16, name="%s_%d" % (name, c))
-                nc.sync.dma_start(
-                    out=piece[:],
-                    in_=rows[:, c * width : (c + 1) * width].rearrange("(t p) k -> p t k", p=P),
-                )
-                tiles.append(piece)
-            return tiles
+        def load_row_tile(name, rows, dmas):
+            width = DIM // dmas
+            halves = []
+            for c in range(dmas):
+                piece = keep.tile([P, width], BF16, name="%s_%d" % (name, c))
+                nc.sync.dma_start(out=piece[:], in_=rows[:, c * width : (c + 1) * width])
+                halves += [piece[:, h * K_HALF : (h + 1) * K_HALF] for h in range(width // K_HALF)]
+            return halves
 
-        sources = {"x%d" % a: x_rows[a * PANEL : (a + 1) * PANEL, :] for a in range(X_PANELS)}
+        panel_rows = {"x0": x_rows[:PANEL, :], "x1": x_rows[PANEL:, :]}
         for s in range(W_PANELS):
-            sources["w%d" % s] = w_qkv_tern[s * PANEL : (s + 1) * PANEL, :]
+            panel_rows["w%d" % s] = w_qkv_tern[s * PANEL : (s + 1) * PANEL, :]
+        in_two_dmas = [("x0", 0), ("x1", 1)]
         raw = {}
-        gain_raw = keep.tile([P, Q_COLS // HD], BF16)
-        for i, name in enumerate(["x0", "w0", "x1"] + ["w%d" % s for s in range(1, W_PANELS)]):
-            if i == SPLIT_LOADS - 1:
-                nc.sync.dma_start(out=gain_raw[:], in_=q_gain.partition_broadcast(P))
-            raw[name] = load_panel(name, sources[name], 2 if i < SPLIT_LOADS else 1)
+        gain_bf16 = keep.tile([P, Q_COLS // HD], BF16)
+        for panel in ["x0", "w0", "x1"] + ["w%d" % s for s in range(1, W_PANELS)]:
+            if panel == "w1":
+                nc.sync.dma_start(out=gain_bf16[:], in_=q_gain.partition_broadcast(P))
+            for t in range(2):
+                rows = panel_rows[panel][t * P : (t + 1) * P, :]
+                raw[panel, t] = load_row_tile("%s_%d" % (panel, t), rows, 2 if (panel, t) in in_two_dmas else 1)
 
         position = keep.tile([P, TOKEN_TILES], I32)
         nc.gpsimd.iota(position[:], pattern=[[P, TOKEN_TILES]], base=0, channel_multiplier=1)
         identity = keep.tile([P, P], F32)
         make_identity(nc, identity[:])
         gain = keep.tile([P, Q_COLS // HD], F32)
-        nc.gpsimd.tensor_copy(out=gain[:], in_=gain_raw[:])
+        nc.gpsimd.tensor_copy(out=gain[:], in_=gain_bf16[:])
 
         ratio = ROPE_BASE ** (-2.0 / HD)
         fine = keep.tile([P, TOKEN_TILES, 8], F32)
@@ -81,94 +87,102 @@ def tile_causalselfattention_pa_kernel(tc, x, w_qkv_tern, q_gain, out_0, out_1, 
             nc.vector.tensor_scalar(
                 out=fine[:, :, lo], in0=position[:], scalar1=ratio**lo / (2 * math.pi), scalar2=None, op0=ALU.mult
             )
-        turns = keep.tile([P, TOKEN_TILES, 2, HALF], F32)
+        turns = keep.tile([P, TOKEN_TILES, 2, FREQS], F32)
         for hi in range(8):
             nc.vector.tensor_scalar(
-                out=turns[:, :, 0, 8 * hi : 8 * hi + 8], in0=fine[:], scalar1=ratio ** (8 * hi), scalar2=None, op0=ALU.mult
+                out=turns[:, :, 0, 8 * hi : 8 * hi + 8],
+                in0=fine[:],
+                scalar1=ratio ** (8 * hi),
+                scalar2=None,
+                op0=ALU.mult,
             )
         nc.vector.tensor_scalar(out=turns[:, :, 1, :], in0=turns[:, :, 0, :], scalar1=-0.25, scalar2=None, op0=ALU.add)
-        whole = keep.tile([P, TOKEN_TILES, 2, HALF], I32)
+        whole = keep.tile([P, TOKEN_TILES, 2, FREQS], I32)
         nc.vector.tensor_copy(out=whole[:], in_=turns[:])
-        fraction = keep.tile([P, TOKEN_TILES, 2, HALF], F32)
+        fraction = keep.tile([P, TOKEN_TILES, 2, FREQS], F32)
         nc.vector.tensor_tensor(out=fraction[:], in0=turns[:], in1=whole[:], op=ALU.subtract)
-        half_sine = keep.tile([P, TOKEN_TILES * 2, HALF], F32)
+        half_sine = keep.tile([P, TOKEN_TILES * 2, FREQS], F32)
         nc.scalar.activation(
             out=half_sine[:], in_=fraction[:].rearrange("p t c j -> p (t c) j"), func=ACT.Sin, scale=math.pi
         )
-        doubled = keep.tile([P, TOKEN_TILES * 2, HALF], F32)
         table = keep.tile([P, TOKEN_TILES, 2, HD], F32)
 
         def finish_table():
+            cos_less_one = keep.tile([P, TOKEN_TILES * 2, FREQS], F32)
             nc.vector.scalar_tensor_tensor(
-                out=doubled[:], in0=half_sine[:], scalar=-2.0, in1=half_sine[:], op0=ALU.mult, op1=ALU.mult
+                out=cos_less_one[:], in0=half_sine[:], scalar=-2.0, in1=half_sine[:], op0=ALU.mult, op1=ALU.mult
             )
             nc.vector.tensor_scalar(
                 out=table[:].rearrange("p t c (d j) -> p (t c) d j", d=2),
-                in0=doubled[:].unsqueeze(2).to_broadcast([P, TOKEN_TILES * 2, 2, HALF]),
+                in0=cos_less_one[:].unsqueeze(2).to_broadcast([P, TOKEN_TILES * 2, 2, FREQS]),
                 scalar1=1.0,
                 scalar2=None,
                 op0=ALU.add,
             )
 
-        def transpose_panel(i):
+        sorted_words = {}
+
+        def sort_words(panel, pieces):
+            for t, half in pieces:
+                words = keep.tile([P, 2, 2, P], F32, name="sorted_%s_%d_%d" % (panel, t, half))
+                nc.vector.tensor_copy(
+                    out=words[:], in_=raw[panel, t][half].bitcast(F32).rearrange("r (g p u) -> r g u p", g=2, u=2)
+                )
+                sorted_words[panel, t, half] = words
+
+        def transpose_panel(panel, order):
             banks = []
-            for g in range(PASSES):
-                bank = psum.tile([P, 2, 2, P], F32, name="turned%d" % g)
-                per_piece = PASSES // len(raw[i])
-                piece = raw[i][g // per_piece]
-                first = 256 * (g % per_piece)
-                for t in range(2):
-                    words = piece[:, t, :].bitcast(F32)
+            for i, (t, half) in enumerate(order):
+                bank = psum.tile([P, 2, 2, P], F32, name="turned%d" % i)
+                for g in range(2):
                     for u in range(2):
-                        nc.tensor.transpose(bank[:, t, u, :], words[:, first + u : first + 256 : 2], identity[:])
+                        if (panel, t, half) in sorted_words:
+                            words = sorted_words[panel, t, half][:, g, u, :]
+                        else:
+                            words = raw[panel, t][half].bitcast(F32)[:, PASS_WORDS * g + u : PASS_WORDS * (g + 1) : 2]
+                        nc.tensor.transpose(bank[:, g, u, :], words, identity[:])
                 banks.append(bank)
             return banks
 
         def new_staged():
-            return work.tile([P, 2, 4 * PANEL], BF16, name="staged", bufs=4, align_bytes=64)
+            return [work.tile([P, 2, 2, 4 * P], BF16, name="staged", bufs=STAGED_BUFS, align_bytes=64) for half in range(2)]
 
-        def copy_out(bank, staged, g, on_vector):
-            dst = staged[:, g % 2, :].bitcast(F32).rearrange("p (t r u) -> p t r u", t=2, u=2)
-            src = bank[:].rearrange("p t u r -> p t r u")
-            if on_vector:
-                nc.vector.tensor_copy(out=dst, in_=src)
-            else:
-                nc.scalar.copy(out=dst, in_=src)
+        def copy_out(bank, staged, piece, copy):
+            t, half = piece
+            copy(
+                out=staged[half][:, :, t, :].bitcast(F32).rearrange("p g (r u) -> p g r u", u=2),
+                in_=bank[:].rearrange("p g u r -> p g r u"),
+            )
 
         def new_operand(pool, name):
             codes = pool.tile([P, PASSES, PANEL], U32, name=name + "_codes", align_bytes=64)
             scales = pool.tile([P, PASSES, PANEL], U8, name=name + "_scales", align_bytes=64)
             return codes, scales
 
-        def quantize(operand, pair, staged, fmt):
+        def quantize(operand, staged, half, fmt):
             codes, scales = operand
-            both = slice(2 * pair, 2 * pair + 2)
+            passes = slice(2 * half, 2 * half + 2)
             nc.vector.quantize_mx(
-                out=codes[:, both, :].rearrange("p g n -> p (g n)").bitcast(fmt),
-                scales=scales[:, both, :].rearrange("p g n -> p (g n)"),
-                in_=staged[:].rearrange("p g n -> p (g n)"),
+                out=codes[:, passes, :].rearrange("p g n -> p (g n)").bitcast(fmt),
+                scales=scales[:, passes, :].rearrange("p g n -> p (g n)"),
+                in_=staged[half][:].rearrange("p g t n -> p (g t n)"),
             )
 
-        def prepare_panel(name, operand, fmt, on_vector):
-            banks = transpose_panel(name)
-            for pair in range(2):
-                staged = new_staged()
-                for g in (2 * pair, 2 * pair + 1):
-                    copy_out(banks[g], staged, g, on_vector)
-                quantize(operand, pair, staged, fmt)
+        def prepare_panel(panel, operand, fmt):
+            banks = transpose_panel(panel, BY_ROWS)
+            staged = new_staged()
+            for bank, (t, half) in zip(banks, BY_ROWS):
+                copy_out(bank, staged, (t, half), nc.scalar.copy)
+                if t == 1:
+                    quantize(operand, staged, half, fmt)
 
-        x_ops = [new_operand(keep, "x%d" % a) for a in range(X_PANELS)]
-        w_ops = {}
-        prepare_panel("x0", x_ops[0], E5M2, False)
-        w_ops[0] = new_operand(work, "w")
-        prepare_panel("w0", w_ops[0], E4M3, False)
-        finish_table()
-        prepare_panel("x1", x_ops[1], E5M2, False)
+        x_operands = [new_operand(keep, "x0"), new_operand(keep, "x1")]
+        w_operands = {}
 
-        def multiply_tile(acc, s, tile):
-            x_codes, x_scales = x_ops[tile // 2]
-            w_codes, w_scales = w_ops[s]
-            tokens = slice(tile % 2 * P, (tile % 2 + 1) * P)
+        def multiply_tile(acc, s, token_tile):
+            x_codes, x_scales = x_operands[token_tile // 2]
+            w_codes, w_scales = w_operands[s]
+            tokens = slice(token_tile % 2 * P, (token_tile % 2 + 1) * P)
             for g in range(PASSES):
                 nc.tensor.matmul_mx(
                     out=acc,
@@ -184,127 +198,152 @@ def tile_causalselfattention_pa_kernel(tc, x, w_qkv_tern, q_gain, out_0, out_1, 
             acc = psum.tile([P, 2, PANEL], F32, name="acc%d" % (2 * (s % 2) + a))
             for t in range(2):
                 multiply_tile(acc[:, t, :], s, 2 * a + t)
-            return {"s": s, "a": a, "acc": acc, "normed": s < QK_PANELS}
+            return {"s": s, "a": a, "acc": acc, "vectors": acc[:].rearrange("p t (h d) -> p (t h) d", d=HD)}
 
-        def sum_squares(job):
-            if not job["normed"]:
-                return
-            squares = work.tile([P, 4, HD], BF16, name="squares")
-            job["sums"] = work.tile([P, 4], F32, name="sums")
-            heads = job["acc"][:].rearrange("p t (h d) -> p (t h) d", d=HD)
-            for c in range(4):
+        def sum_squares(job, sums):
+            squares = work.tile([P, VECTORS, HD], BF16, name="squares")
+            for c in range(VECTORS):
                 nc.scalar.activation(
-                    out=squares[:, c, :], in_=heads[:, c, :], func=ACT.Square, accum_out=job["sums"][:, c : c + 1]
+                    out=squares[:, c, :], in_=job["vectors"][:, c, :], func=ACT.Square, accum_out=sums[:, c : c + 1]
                 )
 
-        def inverse_rms(job):
-            if not job["normed"]:
-                return
-            job["factor"] = work.tile([P, 4], F32, name="inv_rms")
-            nc.scalar.activation(
-                out=job["factor"][:], in_=job["sums"][:], func=ACT.Abs_reciprocal_sqrt, scale=1.0 / HD, bias=RMS_EPS
-            )
+        def inverse_rms(sums):
+            factor = work.tile(list(sums.shape), F32, name="inverse_rms")
+            nc.scalar.activation(out=factor[:], in_=sums, func=ACT.Abs_reciprocal_sqrt, scale=1.0 / HD, bias=RMS_EPS)
+            return factor[:]
 
-        def apply_gain(job):
-            if job["s"] >= Q_PANELS:
-                return
-            gained = work.tile([P, 2, 2], F32, name="gained")
-            factor = job["factor"][:].rearrange("p (t h) -> p t h", t=2)
+        def apply_gain(factor, s):
+            if s >= Q_PANELS:
+                return factor
+            gained = work.tile(list(factor.shape), F32, name="gained")
             for h in range(2):
-                head = 2 * job["s"] + h
+                head = 2 * s + h
                 nc.scalar.activation(
-                    out=gained[:, :, h], in_=factor[:, :, h], func=ACT.Copy, scale=gain[:, head : head + 1]
+                    out=gained[:, h::2], in_=factor[:, h::2], func=ACT.Copy, scale=gain[:, head : head + 1]
                 )
-            job["factor"] = gained[:].rearrange("p t h -> p (t h)")
+            return gained[:]
 
-        def rotate_products(job):
-            job["result"] = keep.tile([P, 2, PANEL], F32, name="result%d_%d" % (job["s"], job["a"]))
-            if not job["normed"]:
-                if job["a"] == 0:
-                    nc.scalar.copy(out=job["result"][:], in_=job["acc"][:])
-                else:
-                    nc.vector.tensor_copy(out=job["result"][:], in_=job["acc"][:])
-                return
-            job["terms"] = work.tile([P, 4, 2, HD], F32, name="terms")
-            heads = job["acc"][:].rearrange("p t (h d) -> p (t h) d", d=HD)
-            for c in range(4):
+        def rotation_terms(job, factor):
+            job["terms"] = work.tile([P, VECTORS, 2, HD], F32, name="terms")
+            for c in range(VECTORS):
                 nc.vector.scalar_tensor_tensor(
                     out=job["terms"][:, c, :, :],
-                    in0=heads[:, c, :].unsqueeze(1).to_broadcast([P, 2, HD]),
-                    scalar=job["factor"][:, c : c + 1],
+                    in0=job["vectors"][:, c, :].unsqueeze(1).to_broadcast([P, 2, HD]),
+                    scalar=factor[:, c : c + 1],
                     in1=table[:, 2 * job["a"] + c // 2, :, :],
                     op0=ALU.mult,
                     op1=ALU.mult,
                 )
 
-        def add_and_store(job):
+        def new_result():
+            return work.tile([P, 2, PANEL], F32, name="result", bufs=RESULT_BUFS)
+
+        def add_terms(job, engine):
+            job["result"] = new_result()
+            terms = job["terms"][:].rearrange("p c f (e j) -> p c (f e) j", e=2)
+            new = job["result"][:].rearrange("p t (h e j) -> p (t h) e j", h=2, e=2)
+            engine.tensor_tensor(out=new[:, :, 0, :], in0=terms[:, :, 0, :], in1=terms[:, :, 3, :], op=ALU.add)
+            engine.tensor_tensor(out=new[:, :, 1, :], in0=terms[:, :, 1, :], in1=terms[:, :, 2, :], op=ALU.subtract)
+
+        def store(job):
             s, a = job["s"], job["a"]
-            if job["normed"]:
-                terms = job["terms"][:].rearrange("p c f (e j) -> p c (f e) j", e=2)
-                halves = job["result"][:].rearrange("p t (h e j) -> p (t h) e j", h=2, e=2)
-                nc.gpsimd.tensor_tensor(out=halves[:, :, 0, :], in0=terms[:, :, 0, :], in1=terms[:, :, 3, :], op=ALU.add)
-                nc.gpsimd.tensor_tensor(
-                    out=halves[:, :, 1, :], in0=terms[:, :, 1, :], in1=terms[:, :, 2, :], op=ALU.subtract
-                )
             if s < Q_PANELS:
                 target, column = q_out, s * PANEL
-            elif s < QK_PANELS:
+            elif s < NORMED_PANELS:
                 target, column = k_out, (s - Q_PANELS) * PANEL
             else:
-                target, column = v_out, (s - QK_PANELS) * PANEL
+                target, column = v_out, (s - NORMED_PANELS) * PANEL
             nc.sync.dma_start(
                 out=target[a * PANEL : (a + 1) * PANEL, column : column + PANEL].rearrange("(t p) c -> p t c", p=P),
                 in_=job["result"][:],
             )
 
-        def statistics(job):
-            sum_squares(job)
-            inverse_rms(job)
-            apply_gain(job)
+        def rotate_and_store(job, factor):
+            rotation_terms(job, factor)
+            add_terms(job, nc.gpsimd)
+            store(job)
 
-        early = multiply(0, 0)
-        statistics(early)
-        w_ops[1] = new_operand(work, "w")
-        prepare_panel("w1", w_ops[1], E4M3, True)
-        late = multiply(0, 1)
-        for s in range(1, W_PANELS):
-            ahead = s + 1 < W_PANELS
-            if ahead:
-                banks = transpose_panel("w%d" % (s + 1))
-                w_ops[s + 1] = new_operand(work, "w")
-                staged = [new_staged(), new_staged()]
+        def new_sums(jobs):
+            return work.tile([P, jobs * VECTORS], F32, name="sums")
 
-            def stage(g):
-                if ahead:
-                    copy_out(banks[g], staged[g // 2], g, False)
+        def begin_panel(s):
+            w_operands[s] = new_operand(work, "w")
+            return transpose_panel("w%d" % s, BY_HALVES), new_staged()
 
-            def quantize_ahead(pair):
-                if ahead:
-                    quantize(w_ops[s + 1], pair, staged[pair], E4M3)
+        def multiply_panel(s):
+            first, second = multiply(s, 0), multiply(s, 1)
+            sums = new_sums(1)
+            sum_squares(first, sums[:])
+            return first, second, apply_gain(inverse_rms(sums[:]), s)
 
-            rotate_products(early)
-            add_and_store(early)
-            sum_squares(late)
-            stage(0)
-            inverse_rms(late)
-            stage(1)
-            apply_gain(late)
-            stage(2)
-            stage(3)
-            quantize_ahead(0)
-            rotate_products(late)
-            add_and_store(late)
-            quantize_ahead(1)
-            early = multiply(s, 0)
-            if ahead:
-                late = multiply(s, 1)
-                statistics(early)
+        w_operands[0] = new_operand(work, "w")
+        w_operands[1] = new_operand(work, "w")
+        prepare_panel("x0", x_operands[0], E5M2)
+        prepare_panel("w0", w_operands[0], E4M3)
+        finish_table()
+        sort_words("w1", BY_ROWS[:2])
+        prepare_panel("x1", x_operands[1], E5M2)
+        sort_words("w1", BY_ROWS[2:])
+        first = multiply(0, 0)
+        sort_words("w2", BY_HALVES)
+        prepare_panel("w1", w_operands[1], E4M3)
+        second = multiply(0, 1)
 
-        rotate_products(early)
-        add_and_store(early)
-        for tile in (2, 3):
-            acc = psum.tile([P, PANEL], F32, name="turned%d" % tile)
-            multiply_tile(acc[:], W_PANELS - 1, tile)
-            result = keep.tile([P, PANEL], F32, name="last%d" % tile)
+        banks, staged = begin_panel(2)
+        sums = new_sums(2)
+        sum_squares(first, sums[:, :VECTORS])
+        sum_squares(second, sums[:, VECTORS:])
+        factors = apply_gain(inverse_rms(sums[:]), 0)
+        for bank, piece in zip(banks, BY_HALVES):
+            copy_out(bank, staged, piece, nc.vector.tensor_copy)
+        quantize(w_operands[2], staged, 0, E4M3)
+        rotate_and_store(first, factors[:, :VECTORS])
+        quantize(w_operands[2], staged, 1, E4M3)
+        rotate_and_store(second, factors[:, VECTORS:])
+        first, second, first_factor = multiply_panel(1)
+
+        def second_factor_among_copies(s, banks, staged, second):
+            sums = new_sums(1)
+            sum_squares(second, sums[:])
+            copy_out(banks[0], staged, BY_HALVES[0], nc.scalar.copy)
+            factor = inverse_rms(sums[:])
+            copy_out(banks[1], staged, BY_HALVES[1], nc.scalar.copy)
+            factor = apply_gain(factor, s - 1)
+            copy_out(banks[2], staged, BY_HALVES[2], nc.scalar.copy)
+            copy_out(banks[3], staged, BY_HALVES[3], nc.scalar.copy)
+            return factor
+
+        for s in range(2, NORMED_PANELS):
+            banks, staged = begin_panel(s + 1)
+            rotate_and_store(first, first_factor)
+            second_factor = second_factor_among_copies(s, banks, staged, second)
+            quantize(w_operands[s + 1], staged, 0, E4M3)
+            rotate_and_store(second, second_factor)
+            quantize(w_operands[s + 1], staged, 1, E4M3)
+            first, second, first_factor = multiply_panel(s)
+
+        last = W_PANELS - 1
+        banks, staged = begin_panel(last)
+        rotate_and_store(first, first_factor)
+        second_factor = second_factor_among_copies(NORMED_PANELS, banks, staged, second)
+        rotation_terms(second, second_factor)
+        quantize(w_operands[last], staged, 0, E4M3)
+        quantize(w_operands[last], staged, 1, E4M3)
+        add_terms(second, nc.vector)
+
+        def v_job(s, a):
+            job = multiply(s, a)
+            job["result"] = new_result()
+            nc.scalar.copy(out=job["result"][:], in_=job["acc"][:])
+            store(job)
+
+        v_job(last - 1, 0)
+        store(second)
+        v_job(last - 1, 1)
+        v_job(last, 0)
+        for token_tile in (2, 3):
+            acc = psum.tile([P, PANEL], F32, name="turned%d" % token_tile)
+            multiply_tile(acc[:], last, token_tile)
+            result = keep.tile([P, PANEL], F32, name="v_tile%d" % token_tile)
             nc.vector.tensor_copy(out=result[:], in_=acc[:])
-            nc.sync.dma_start(out=v_out[tile * P : (tile + 1) * P, V_COLS - PANEL :], in_=result[:])
+            nc.sync.dma_start(out=v_out[token_tile * P : (token_tile + 1) * P, V_COLS - PANEL :], in_=result[:])

@@ -36,7 +36,7 @@ BY_ROWS = [(0, 0), (0, 1), (1, 0), (1, 1)]
 BY_HALVES = [(0, 0), (1, 0), (0, 1), (1, 1)]
 
 STAGED_BUFS = 4
-RESULT_BUFS = 12
+EARLY_VECTORS = VECTORS - 1
 
 
 def tile_causalselfattention_pa_kernel(tc, x, w_qkv_tern, q_gain, out_0, out_1, out_2):
@@ -120,27 +120,15 @@ def tile_causalselfattention_pa_kernel(tc, x, w_qkv_tern, q_gain, out_0, out_1, 
                 op0=ALU.add,
             )
 
-        sorted_words = {}
-
-        def sort_words(panel, pieces):
-            for t, half in pieces:
-                words = keep.tile([P, 2, 2, P], F32, name="sorted_%s_%d_%d" % (panel, t, half))
-                nc.vector.tensor_copy(
-                    out=words[:], in_=raw[panel, t][half].bitcast(F32).rearrange("r (g p u) -> r g u p", g=2, u=2)
-                )
-                sorted_words[panel, t, half] = words
-
         def transpose_panel(panel, order):
             banks = []
             for i, (t, half) in enumerate(order):
                 bank = psum.tile([P, 2, 2, P], F32, name="turned%d" % i)
+                words = raw[panel, t][half].bitcast(F32)
                 for g in range(2):
                     for u in range(2):
-                        if (panel, t, half) in sorted_words:
-                            words = sorted_words[panel, t, half][:, g, u, :]
-                        else:
-                            words = raw[panel, t][half].bitcast(F32)[:, PASS_WORDS * g + u : PASS_WORDS * (g + 1) : 2]
-                        nc.tensor.transpose(bank[:, g, u, :], words, identity[:])
+                        every_second = words[:, PASS_WORDS * g + u : PASS_WORDS * (g + 1) : 2]
+                        nc.tensor.transpose(bank[:, g, u, :], every_second, identity[:])
                 banks.append(bank)
             return banks
 
@@ -168,11 +156,11 @@ def tile_causalselfattention_pa_kernel(tc, x, w_qkv_tern, q_gain, out_0, out_1, 
                 in_=staged[half][:].rearrange("p g t n -> p (g t n)"),
             )
 
-        def prepare_panel(panel, operand, fmt):
+        def prepare_panel(panel, operand, fmt, copy):
             banks = transpose_panel(panel, BY_ROWS)
             staged = new_staged()
             for bank, (t, half) in zip(banks, BY_ROWS):
-                copy_out(bank, staged, (t, half), nc.scalar.copy)
+                copy_out(bank, staged, (t, half), copy)
                 if t == 1:
                     quantize(operand, staged, half, fmt)
 
@@ -198,52 +186,51 @@ def tile_causalselfattention_pa_kernel(tc, x, w_qkv_tern, q_gain, out_0, out_1, 
             acc = psum.tile([P, 2, PANEL], F32, name="acc%d" % (2 * (s % 2) + a))
             for t in range(2):
                 multiply_tile(acc[:, t, :], s, 2 * a + t)
-            return {"s": s, "a": a, "acc": acc, "vectors": acc[:].rearrange("p t (h d) -> p (t h) d", d=HD)}
+            result = keep.tile([P, 2, PANEL], F32, name="result%d_%d" % (s, a))
+            vectors = acc[:].rearrange("p t (h d) -> p (t h) d", d=HD)
+            return {"s": s, "a": a, "acc": acc, "vectors": vectors, "result": result}
 
-        def sum_squares(job, sums):
+        def sum_squares(job):
             squares = work.tile([P, VECTORS, HD], BF16, name="squares")
+            sums = work.tile([P, VECTORS], F32, name="sums")
             for c in range(VECTORS):
                 nc.scalar.activation(
                     out=squares[:, c, :], in_=job["vectors"][:, c, :], func=ACT.Square, accum_out=sums[:, c : c + 1]
                 )
+            return sums
 
         def inverse_rms(sums):
-            factor = work.tile(list(sums.shape), F32, name="inverse_rms")
-            nc.scalar.activation(out=factor[:], in_=sums, func=ACT.Abs_reciprocal_sqrt, scale=1.0 / HD, bias=RMS_EPS)
-            return factor[:]
+            factor = work.tile([P, VECTORS], F32, name="inverse_rms")
+            nc.scalar.activation(out=factor[:], in_=sums[:], func=ACT.Abs_reciprocal_sqrt, scale=1.0 / HD, bias=RMS_EPS)
+            return factor
 
-        def apply_gain(factor, s):
-            if s >= Q_PANELS:
-                return factor
-            gained = work.tile(list(factor.shape), F32, name="gained")
-            for h in range(2):
-                head = 2 * s + h
-                nc.scalar.activation(
-                    out=gained[:, h::2], in_=factor[:, h::2], func=ACT.Copy, scale=gain[:, head : head + 1]
-                )
-            return gained[:]
+        def apply_gain(job, factor):
+            job["factor"] = factor
+            if job["s"] < Q_PANELS:
+                job["factor"] = work.tile([P, VECTORS], F32, name="gained")
+                for h in range(2):
+                    head = 2 * job["s"] + h
+                    nc.scalar.activation(
+                        out=job["factor"][:, h::2], in_=factor[:, h::2], func=ACT.Copy, scale=gain[:, head : head + 1]
+                    )
 
-        def rotation_terms(job, factor):
-            job["terms"] = work.tile([P, VECTORS, 2, HD], F32, name="terms")
-            for c in range(VECTORS):
+        def rotation_terms(job, vectors):
+            for c in vectors:
                 nc.vector.scalar_tensor_tensor(
                     out=job["terms"][:, c, :, :],
                     in0=job["vectors"][:, c, :].unsqueeze(1).to_broadcast([P, 2, HD]),
-                    scalar=factor[:, c : c + 1],
+                    scalar=job["factor"][:, c : c + 1],
                     in1=table[:, 2 * job["a"] + c // 2, :, :],
                     op0=ALU.mult,
                     op1=ALU.mult,
                 )
 
-        def new_result():
-            return work.tile([P, 2, PANEL], F32, name="result", bufs=RESULT_BUFS)
-
-        def add_terms(job, engine):
-            job["result"] = new_result()
+        def add_terms(job, e, engine):
             terms = job["terms"][:].rearrange("p c f (e j) -> p c (f e) j", e=2)
             new = job["result"][:].rearrange("p t (h e j) -> p (t h) e j", h=2, e=2)
-            engine.tensor_tensor(out=new[:, :, 0, :], in0=terms[:, :, 0, :], in1=terms[:, :, 3, :], op=ALU.add)
-            engine.tensor_tensor(out=new[:, :, 1, :], in0=terms[:, :, 1, :], in1=terms[:, :, 2, :], op=ALU.subtract)
+            engine.tensor_tensor(
+                out=new[:, :, e, :], in0=terms[:, :, e, :], in1=terms[:, :, 3 - e, :], op=(ALU.add, ALU.subtract)[e]
+            )
 
         def store(job):
             s, a = job["s"], job["a"]
@@ -258,88 +245,64 @@ def tile_causalselfattention_pa_kernel(tc, x, w_qkv_tern, q_gain, out_0, out_1, 
                 in_=job["result"][:],
             )
 
-        def rotate_and_store(job, factor):
-            rotation_terms(job, factor)
-            add_terms(job, nc.gpsimd)
-            store(job)
+        def rotate(job, job_before, quantize_calls, first_sum_on):
+            job["terms"] = work.tile([P, VECTORS, 2, HD], F32, name="terms")
+            rotation_terms(job, range(EARLY_VECTORS))
+            if job_before:
+                add_terms(job_before, 1, nc.vector)
+                store(job_before)
+            for s, staged, half in quantize_calls:
+                quantize(w_operands[s], staged, half, E4M3)
+            rotation_terms(job, range(EARLY_VECTORS, VECTORS))
+            add_terms(job, 0, first_sum_on)
 
-        def new_sums(jobs):
-            return work.tile([P, jobs * VECTORS], F32, name="sums")
-
-        def begin_panel(s):
-            w_operands[s] = new_operand(work, "w")
-            return transpose_panel("w%d" % s, BY_HALVES), new_staged()
-
-        def multiply_panel(s):
-            first, second = multiply(s, 0), multiply(s, 1)
-            sums = new_sums(1)
-            sum_squares(first, sums[:])
-            return first, second, apply_gain(inverse_rms(sums[:]), s)
+        def begin_step(s, second):
+            w_operands[s + 1] = new_operand(work, "w")
+            banks = transpose_panel("w%d" % (s + 1), BY_HALVES)
+            staged = new_staged()
+            sums = sum_squares(second)
+            copy_out(banks[0], staged, BY_HALVES[0], nc.scalar.copy)
+            factor = inverse_rms(sums)
+            copy_out(banks[1], staged, BY_HALVES[1], nc.scalar.copy)
+            apply_gain(second, factor)
+            copy_out(banks[2], staged, BY_HALVES[2], nc.scalar.copy)
+            copy_out(banks[3], staged, BY_HALVES[3], nc.scalar.copy)
+            return staged
 
         w_operands[0] = new_operand(work, "w")
         w_operands[1] = new_operand(work, "w")
-        prepare_panel("x0", x_operands[0], E5M2)
-        prepare_panel("w0", w_operands[0], E4M3)
+        prepare_panel("x0", x_operands[0], E5M2, nc.scalar.copy)
+        prepare_panel("w0", w_operands[0], E4M3, nc.scalar.copy)
         finish_table()
-        sort_words("w1", BY_ROWS[:2])
-        prepare_panel("x1", x_operands[1], E5M2)
-        sort_words("w1", BY_ROWS[2:])
+        prepare_panel("x1", x_operands[1], E5M2, nc.scalar.copy)
         first = multiply(0, 0)
-        sort_words("w2", BY_HALVES)
-        prepare_panel("w1", w_operands[1], E4M3)
+        apply_gain(first, inverse_rms(sum_squares(first)))
+        prepare_panel("w1", w_operands[1], E4M3, nc.vector.tensor_copy)
         second = multiply(0, 1)
 
-        banks, staged = begin_panel(2)
-        sums = new_sums(2)
-        sum_squares(first, sums[:, :VECTORS])
-        sum_squares(second, sums[:, VECTORS:])
-        factors = apply_gain(inverse_rms(sums[:]), 0)
-        for bank, piece in zip(banks, BY_HALVES):
-            copy_out(bank, staged, piece, nc.vector.tensor_copy)
-        quantize(w_operands[2], staged, 0, E4M3)
-        rotate_and_store(first, factors[:, :VECTORS])
-        quantize(w_operands[2], staged, 1, E4M3)
-        rotate_and_store(second, factors[:, VECTORS:])
-        first, second, first_factor = multiply_panel(1)
-
-        def second_factor_among_copies(s, banks, staged, second):
-            sums = new_sums(1)
-            sum_squares(second, sums[:])
-            copy_out(banks[0], staged, BY_HALVES[0], nc.scalar.copy)
-            factor = inverse_rms(sums[:])
-            copy_out(banks[1], staged, BY_HALVES[1], nc.scalar.copy)
-            factor = apply_gain(factor, s - 1)
-            copy_out(banks[2], staged, BY_HALVES[2], nc.scalar.copy)
-            copy_out(banks[3], staged, BY_HALVES[3], nc.scalar.copy)
-            return factor
-
-        for s in range(2, NORMED_PANELS):
-            banks, staged = begin_panel(s + 1)
-            rotate_and_store(first, first_factor)
-            second_factor = second_factor_among_copies(s, banks, staged, second)
-            quantize(w_operands[s + 1], staged, 0, E4M3)
-            rotate_and_store(second, second_factor)
-            quantize(w_operands[s + 1], staged, 1, E4M3)
-            first, second, first_factor = multiply_panel(s)
+        unfinished = None
+        for s in range(1, NORMED_PANELS):
+            staged = begin_step(s, second)
+            rotate(first, unfinished, [(s + 1, staged, 0)], nc.gpsimd)
+            rotate(second, first, [(s + 1, staged, 1)], nc.gpsimd)
+            unfinished = second
+            first, second = multiply(s, 0), multiply(s, 1)
+            apply_gain(first, inverse_rms(sum_squares(first)))
 
         last = W_PANELS - 1
-        banks, staged = begin_panel(last)
-        rotate_and_store(first, first_factor)
-        second_factor = second_factor_among_copies(NORMED_PANELS, banks, staged, second)
-        rotation_terms(second, second_factor)
-        quantize(w_operands[last], staged, 0, E4M3)
-        quantize(w_operands[last], staged, 1, E4M3)
-        add_terms(second, nc.vector)
+        staged = begin_step(NORMED_PANELS, second)
+        rotate(first, unfinished, [], nc.gpsimd)
+        rotate(second, first, [(last, staged, 0), (last, staged, 1)], nc.vector)
+        add_terms(second, 1, nc.vector)
 
         def v_job(s, a):
             job = multiply(s, a)
-            job["result"] = new_result()
             nc.scalar.copy(out=job["result"][:], in_=job["acc"][:])
             store(job)
 
         v_job(last - 1, 0)
-        store(second)
         v_job(last - 1, 1)
+        store(second)
         v_job(last, 0)
         for token_tile in (2, 3):
             acc = psum.tile([P, PANEL], F32, name="turned%d" % token_tile)

import math
from contextlib import ExitStack

import concourse.mybir as mybir
from concourse.masks import make_identity

S, DIM, HD = 512, 2048, 128
Q_COLS, K_COLS, V_COLS = 2048, 512, 512
ROPE_BASE = 10000.0
RMS_EPS = 1.1920929e-07
FLOPS = 2 * S * DIM * (Q_COLS + K_COLS + V_COLS)

F32 = mybir.dt.float32
BF16 = mybir.dt.bfloat16
I32 = mybir.dt.int32
U32 = mybir.dt.uint32
U8 = mybir.dt.uint8
E5M2 = mybir.dt.float8_e5m2_x4
E4M3 = mybir.dt.float8_e4m3fn_x4
ALU = mybir.AluOpType
ACT = mybir.ActivationFunctionType

P = 128
FREQS = HD // 2
PASSES = DIM // 512
PASS_WORDS = 256
K_HALF = DIM // 2
PANEL = 2 * P
TOKEN_TILES = S // P
Q_PANELS = Q_COLS // PANEL
NORMED_PANELS = (Q_COLS + K_COLS) // PANEL
W_PANELS = (Q_COLS + K_COLS + V_COLS) // PANEL
VECTORS = 4

BY_ROWS = [(0, 0), (0, 1), (1, 0), (1, 1)]
BY_HALVES = [(0, 0), (1, 0), (0, 1), (1, 1)]

STAGED_BUFS = 4
EARLY_VECTORS = VECTORS - 1


def tile_causalselfattention_pa_kernel(tc, x, w_qkv_tern, q_gain, out_0, out_1, out_2):
    nc = tc.nc
    x_rows = x.rearrange("b s k -> (b s) k")
    q_out = out_0.rearrange("b s h d -> (b s) (h d)")
    k_out = out_1.rearrange("b s h d -> (b s) (h d)")
    v_out = out_2.rearrange("b s h d -> (b s) (h d)")

    with ExitStack() as ctx:
        keep = ctx.enter_context(tc.tile_pool(name="keep", bufs=1))
        work = ctx.enter_context(tc.tile_pool(name="work", bufs=3))
        psum = ctx.enter_context(tc.psum_pool(name="psum", bufs=1))
        ctx.enter_context(tc.manual_schedule())

        def load_row_tile(name, rows, dmas):
            width = DIM // dmas
            halves = []
            for c in range(dmas):
                piece = keep.tile([P, width], BF16, name="%s_%d" % (name, c))
                nc.sync.dma_start(out=piece[:], in_=rows[:, c * width : (c + 1) * width])
                halves += [piece[:, h * K_HALF : (h + 1) * K_HALF] for h in range(width // K_HALF)]
            return halves

        panel_rows = {"x0": x_rows[:PANEL, :], "x1": x_rows[PANEL:, :]}
        for s in range(W_PANELS):
            panel_rows["w%d" % s] = w_qkv_tern[s * PANEL : (s + 1) * PANEL, :]
        in_two_dmas = [("x0", 0), ("x1", 1)]
        raw = {}
        gain_bf16 = keep.tile([P, Q_COLS // HD], BF16)
        for panel in ["x0", "w0", "x1"] + ["w%d" % s for s in range(1, W_PANELS)]:
            if panel == "w1":
                nc.sync.dma_start(out=gain_bf16[:], in_=q_gain.partition_broadcast(P))
            for t in range(2):
                rows = panel_rows[panel][t * P : (t + 1) * P, :]
                raw[panel, t] = load_row_tile("%s_%d" % (panel, t), rows, 2 if (panel, t) in in_two_dmas else 1)

        position = keep.tile([P, TOKEN_TILES], I32)
        nc.gpsimd.iota(position[:], pattern=[[P, TOKEN_TILES]], base=0, channel_multiplier=1)
        identity = keep.tile([P, P], F32)
        make_identity(nc, identity[:])
        gain = keep.tile([P, Q_COLS // HD], F32)
        nc.gpsimd.tensor_copy(out=gain[:], in_=gain_bf16[:])

        ratio = ROPE_BASE ** (-2.0 / HD)
        fine = keep.tile([P, TOKEN_TILES, 8], F32)
        for lo in range(8):
            nc.vector.tensor_scalar(
                out=fine[:, :, lo], in0=position[:], scalar1=ratio**lo / (2 * math.pi), scalar2=None, op0=ALU.mult
            )
        turns = keep.tile([P, TOKEN_TILES, 2, FREQS], F32)
        for hi in range(8):
            nc.vector.tensor_scalar(
                out=turns[:, :, 0, 8 * hi : 8 * hi + 8],
                in0=fine[:],
                scalar1=ratio ** (8 * hi),
                scalar2=None,
                op0=ALU.mult,
            )
        nc.vector.tensor_scalar(out=turns[:, :, 1, :], in0=turns[:, :, 0, :], scalar1=-0.25, scalar2=None, op0=ALU.add)
        whole = keep.tile([P, TOKEN_TILES, 2, FREQS], I32)
        nc.vector.tensor_copy(out=whole[:], in_=turns[:])
        fraction = keep.tile([P, TOKEN_TILES, 2, FREQS], F32)
        nc.vector.tensor_tensor(out=fraction[:], in0=turns[:], in1=whole[:], op=ALU.subtract)
        half_sine = keep.tile([P, TOKEN_TILES * 2, FREQS], F32)
        nc.scalar.activation(
            out=half_sine[:], in_=fraction[:].rearrange("p t c j -> p (t c) j"), func=ACT.Sin, scale=math.pi
        )
        table = keep.tile([P, TOKEN_TILES, 2, HD], F32)

        def finish_table():
            cos_less_one = keep.tile([P, TOKEN_TILES * 2, FREQS], F32)
            nc.vector.scalar_tensor_tensor(
                out=cos_less_one[:], in0=half_sine[:], scalar=-2.0, in1=half_sine[:], op0=ALU.mult, op1=ALU.mult
            )
            nc.vector.tensor_scalar(
                out=table[:].rearrange("p t c (d j) -> p (t c) d j", d=2),
                in0=cos_less_one[:].unsqueeze(2).to_broadcast([P, TOKEN_TILES * 2, 2, FREQS]),
                scalar1=1.0,
                scalar2=None,
                op0=ALU.add,
            )

        def transpose_panel(panel, order):
            banks = []
            for i, (t, half) in enumerate(order):
                bank = psum.tile([P, 2, 2, P], F32, name="turned%d" % i)
                words = raw[panel, t][half].bitcast(F32)
                for g in range(2):
                    for u in range(2):
                        every_second = words[:, PASS_WORDS * g + u : PASS_WORDS * (g + 1) : 2]
                        nc.tensor.transpose(bank[:, g, u, :], every_second, identity[:])
                banks.append(bank)
            return banks

        def new_staged():
            return [work.tile([P, 2, 2, 4 * P], BF16, name="staged", bufs=STAGED_BUFS, align_bytes=64) for half in range(2)]

        def copy_out(bank, staged, piece, copy):
            t, half = piece
            copy(
                out=staged[half][:, :, t, :].bitcast(F32).rearrange("p g (r u) -> p g r u", u=2),
                in_=bank[:].rearrange("p g u r -> p g r u"),
            )

        def new_operand(pool, name):
            codes = pool.tile([P, PASSES, PANEL], U32, name=name + "_codes", align_bytes=64)
            scales = pool.tile([P, PASSES, PANEL], U8, name=name + "_scales", align_bytes=64)
            return codes, scales

        def quantize(operand, staged, half, fmt):
            codes, scales = operand
            passes = slice(2 * half, 2 * half + 2)
            nc.vector.quantize_mx(
                out=codes[:, passes, :].rearrange("p g n -> p (g n)").bitcast(fmt),
                scales=scales[:, passes, :].rearrange("p g n -> p (g n)"),
                in_=staged[half][:].rearrange("p g t n -> p (g t n)"),
            )

        def prepare_panel(panel, operand, fmt, copy):
            banks = transpose_panel(panel, BY_ROWS)
            staged = new_staged()
            for bank, (t, half) in zip(banks, BY_ROWS):
                copy_out(bank, staged, (t, half), copy)
                if t == 1:
                    quantize(operand, staged, half, fmt)

        x_operands = [new_operand(keep, "x0"), new_operand(keep, "x1")]
        w_operands = {}

        def multiply_tile(acc, s, token_tile):
            x_codes, x_scales = x_operands[token_tile // 2]
            w_codes, w_scales = w_operands[s]
            tokens = slice(token_tile % 2 * P, (token_tile % 2 + 1) * P)
            for g in range(PASSES):
                nc.tensor.matmul_mx(
                    out=acc,
                    lhsT=x_codes[:, g, tokens].bitcast(E5M2),
                    lhsT_scale=x_scales[:, g, tokens],
                    rhs=w_codes[:, g, :].bitcast(E4M3),
                    rhs_scale=w_scales[:, g, :],
                    start=(g == 0),
                    stop=(g == PASSES - 1),
                )

        def multiply(s, a):
            acc = psum.tile([P, 2, PANEL], F32, name="acc%d" % (2 * (s % 2) + a))
            for t in range(2):
                multiply_tile(acc[:, t, :], s, 2 * a + t)
            result = keep.tile([P, 2, PANEL], F32, name="result%d_%d" % (s, a))
            vectors = acc[:].rearrange("p t (h d) -> p (t h) d", d=HD)
            return {"s": s, "a": a, "acc": acc, "vectors": vectors, "result": result}

        def sum_squares(job):
            squares = work.tile([P, VECTORS, HD], BF16, name="squares")
            sums = work.tile([P, VECTORS], F32, name="sums")
            for c in range(VECTORS):
                nc.scalar.activation(
                    out=squares[:, c, :], in_=job["vectors"][:, c, :], func=ACT.Square, accum_out=sums[:, c : c + 1]
                )
            return sums

        def inverse_rms(sums):
            factor = work.tile([P, VECTORS], F32, name="inverse_rms")
            nc.scalar.activation(out=factor[:], in_=sums[:], func=ACT.Abs_reciprocal_sqrt, scale=1.0 / HD, bias=RMS_EPS)
            return factor

        def apply_gain(job, factor):
            job["factor"] = factor
            if job["s"] < Q_PANELS:
                job["factor"] = work.tile([P, VECTORS], F32, name="gained")
                for h in range(2):
                    head = 2 * job["s"] + h
                    nc.scalar.activation(
                        out=job["factor"][:, h::2], in_=factor[:, h::2], func=ACT.Copy, scale=gain[:, head : head + 1]
                    )

        def rotation_terms(job, vectors):
            for c in vectors:
                nc.vector.scalar_tensor_tensor(
                    out=job["terms"][:, c, :, :],
                    in0=job["vectors"][:, c, :].unsqueeze(1).to_broadcast([P, 2, HD]),
                    scalar=job["factor"][:, c : c + 1],
                    in1=table[:, 2 * job["a"] + c // 2, :, :],
                    op0=ALU.mult,
                    op1=ALU.mult,
                )

        def add_terms(job, e, engine):
            terms = job["terms"][:].rearrange("p c f (e j) -> p c (f e) j", e=2)
            new = job["result"][:].rearrange("p t (h e j) -> p (t h) e j", h=2, e=2)
            engine.tensor_tensor(
                out=new[:, :, e, :], in0=terms[:, :, e, :], in1=terms[:, :, 3 - e, :], op=(ALU.add, ALU.subtract)[e]
            )

        def store(job):
            s, a = job["s"], job["a"]
            if s < Q_PANELS:
                target, column = q_out, s * PANEL
            elif s < NORMED_PANELS:
                target, column = k_out, (s - Q_PANELS) * PANEL
            else:
                target, column = v_out, (s - NORMED_PANELS) * PANEL
            nc.sync.dma_start(
                out=target[a * PANEL : (a + 1) * PANEL, column : column + PANEL].rearrange("(t p) c -> p t c", p=P),
                in_=job["result"][:],
            )

        def rotate(job, job_before, quantize_calls, first_sum_on):
            job["terms"] = work.tile([P, VECTORS, 2, HD], F32, name="terms")
            rotation_terms(job, range(EARLY_VECTORS))
            if job_before:
                add_terms(job_before, 1, nc.vector)
                store(job_before)
            for s, staged, half in quantize_calls:
                quantize(w_operands[s], staged, half, E4M3)
            rotation_terms(job, range(EARLY_VECTORS, VECTORS))
            add_terms(job, 0, first_sum_on)

        def begin_step(s, second):
            w_operands[s + 1] = new_operand(work, "w")
            banks = transpose_panel("w%d" % (s + 1), BY_HALVES)
            staged = new_staged()
            sums = sum_squares(second)
            copy_out(banks[0], staged, BY_HALVES[0], nc.scalar.copy)
            factor = inverse_rms(sums)
            copy_out(banks[1], staged, BY_HALVES[1], nc.scalar.copy)
            apply_gain(second, factor)
            copy_out(banks[2], staged, BY_HALVES[2], nc.scalar.copy)
            copy_out(banks[3], staged, BY_HALVES[3], nc.scalar.copy)
            return staged

        w_operands[0] = new_operand(work, "w")
        w_operands[1] = new_operand(work, "w")
        prepare_panel("x0", x_operands[0], E5M2, nc.scalar.copy)
        prepare_panel("w0", w_operands[0], E4M3, nc.scalar.copy)
        finish_table()
        prepare_panel("x1", x_operands[1], E5M2, nc.scalar.copy)
        first = multiply(0, 0)
        apply_gain(first, inverse_rms(sum_squares(first)))
        prepare_panel("w1", w_operands[1], E4M3, nc.vector.tensor_copy)
        second = multiply(0, 1)

        unfinished = None
        for s in range(1, NORMED_PANELS):
            staged = begin_step(s, second)
            rotate(first, unfinished, [(s + 1, staged, 0)], nc.gpsimd)
            rotate(second, first, [(s + 1, staged, 1)], nc.gpsimd)
            unfinished = second
            first, second = multiply(s, 0), multiply(s, 1)
            apply_gain(first, inverse_rms(sum_squares(first)))

        last = W_PANELS - 1
        staged = begin_step(NORMED_PANELS, second)
        rotate(first, unfinished, [], nc.gpsimd)
        rotate(second, first, [(last, staged, 0), (last, staged, 1)], nc.vector)
        add_terms(second, 1, nc.vector)

        def v_job(s, a):
            job = multiply(s, a)
            nc.scalar.copy(out=job["result"][:], in_=job["acc"][:])
            store(job)

        v_job(last - 1, 0)
        v_job(last - 1, 1)
        store(second)
        v_job(last, 0)
        for token_tile in (2, 3):
            acc = psum.tile([P, PANEL], F32, name="turned%d" % token_tile)
            multiply_tile(acc[:], last, token_tile)
            result = keep.tile([P, PANEL], F32, name="v_tile%d" % token_tile)
            nc.vector.tensor_copy(out=result[:], in_=acc[:])
            nc.sync.dma_start(out=v_out[token_tile * P : (token_tile + 1) * P, V_COLS - PANEL :], in_=result[:])
